import numpy as np
import ml_dtypes

BF16 = ml_dtypes.bfloat16


def bf(x):
    return np.asarray(x, np.float32).astype(BF16)


def f32(x):
    return np.asarray(x, np.float32)


def f64(x):
    return np.asarray(x).astype(np.float64)


def striped(idx):
    return np.tile(idx.reshape(-1, 16).T, (8, 1))


C, S, N = 256, 4096, 512
EPS = 1e-5


def setup_inputs():
    return {"wte": f32(np.random.standard_normal((C, S))), "wpe": f32(np.random.standard_normal((C, N))), "ln_w": f32(1.0 + 0.1 * np.random.standard_normal((C, 1))), "ln_b": f32(0.1 * np.random.standard_normal((C, 1))), "offs": striped(np.random.permutation(np.tile(np.arange(S), 2))[:N])}


def reference(wte, wpe, ln_w, ln_b, offs):
    idx = offs[:16].T.reshape(-1)
    h = f64(wte)[:, idx] + f64(wpe)
    mu = h.mean(axis=0, keepdims=True)
    var = ((h - mu) ** 2).mean(axis=0, keepdims=True)
    return (h - mu) / np.sqrt(var + EPS) * f64(ln_w) + f64(ln_b)

@@ -1,0 +1,61 @@
+import concourse.mybir as mybir
+
+F32 = mybir.dt.float32
+U16 = mybir.dt.uint16
+ALU = mybir.AluOpType
+ACT = mybir.ActivationFunctionType
+
+P = 128
+C, S, N = 256, 4096, 512
+BLOCKS = C // P
+EPS = 1e-5
+FLOPS = 8 * C * N
+
+
+def tile_gptqbigcodemodel_kernel(tc, wte, wpe, ln_w, ln_b, offs, out):
+    nc = tc.nc
+    with (
+        tc.tile_pool(name="held", bufs=1) as held,
+        tc.psum_pool(name="psum", bufs=1) as psum,
+    ):
+        offsets = held.tile([P, N // 16], U16, name="offsets")
+        nc.sync.dma_start(offsets[:], offs)
+        position, table, gain, bias = [], [], [], []
+        for b in range(BLOCKS):
+            rows = slice(b * P, (b + 1) * P)
+            position.append(held.tile([P, N], F32, name=f"position{b}"))
+            table.append(held.tile([P, S], F32, name=f"table{b}"))
+            gain.append(held.tile([P, 1], F32, name=f"gain{b}"))
+            bias.append(held.tile([P, 1], F32, name=f"bias{b}"))
+            nc.sync.dma_start(position[b][:], wpe[rows, :])
+            nc.sync.dma_start(table[b][:], wte[rows, :])
+            nc.gpsimd.dma_start(gain[b][:], ln_w[rows, :])
+            nc.gpsimd.dma_start(bias[b][:], ln_b[rows, :])
+
+        averager = held.tile([P, P], F32, name="averager")
+        nc.vector.memset(averager[:], 1.0 / C)
+
+        mean = psum.tile([P, N], F32, name="mean")
+        h = []
+        for b in range(BLOCKS):
+            h.append(held.tile([P, N], F32, name=f"h{b}"))
+            nc.vector.tensor_tensor(h[b][:], table[b][:].indirect(offsets[:]), position[b][:], ALU.add)
+            nc.tensor.matmul(mean[:], averager[:], h[b][:], start=(b == 0), stop=(b == BLOCKS - 1))
+
+        variance = psum.tile([P, N], F32, name="variance")
+        centred = []
+        for b in range(BLOCKS):
+            centred.append(held.tile([P, N], F32, name=f"centred{b}"))
+            squared = held.tile([P, N], F32, name=f"squared{b}")
+            nc.vector.tensor_tensor(centred[b][:], h[b][:], mean[:], ALU.subtract)
+            nc.scalar.activation(squared[:], centred[b][:], ACT.Square)
+            nc.tensor.matmul(variance[:], averager[:], squared[:], start=(b == 0), stop=(b == BLOCKS - 1))
+
+        rstd = held.tile([P, N], F32, name="rstd")
+        nc.scalar.activation(rstd[:], variance[:], ACT.Abs_reciprocal_sqrt, bias=EPS)
+        for b in range(BLOCKS):
+            normed = held.tile([P, N], F32, name=f"normed{b}")
+            result = held.tile([P, N], F32, name=f"result{b}")
+            nc.vector.tensor_tensor(normed[:], centred[b][:], rstd[:], ALU.mult)
+            nc.scalar.activation(result[:], normed[:], ACT.Identity, bias=bias[b][:], scale=gain[b][:])
+            nc.sync.dma_start(out[b * P : (b + 1) * P, :], result[:])

@@ -1,6 +1,7 @@
 import concourse.mybir as mybir
 
 F32 = mybir.dt.float32
+BF16 = mybir.dt.bfloat16
 U16 = mybir.dt.uint16
 ALU = mybir.AluOpType
 ACT = mybir.ActivationFunctionType
@@ -8,6 +9,8 @@ ACT = mybir.ActivationFunctionType
 P = 128
 C, S, N = 256, 4096, 512
 BLOCKS = C // P
+PIECES = 4
+T = N // PIECES
 EPS = 1e-5
 FLOPS = 8 * C * N
 
@@ -16,7 +19,9 @@ def tile_gptqbigcodemodel_kernel(tc, wte, wpe, ln_w, ln_b, offs, out):
     nc = tc.nc
     with (
         tc.tile_pool(name="held", bufs=1) as held,
-        tc.psum_pool(name="psum", bufs=1) as psum,
+        tc.tile_pool(name="work", bufs=PIECES) as work,
+        tc.psum_pool(name="mean_banks", bufs=1) as mean_banks,
+        tc.psum_pool(name="variance_banks", bufs=PIECES) as variance_banks,
     ):
         offsets = held.tile([P, N // 16], U16, name="offsets")
         nc.sync.dma_start(offsets[:], offs)
@@ -29,33 +34,47 @@ def tile_gptqbigcodemodel_kernel(tc, wte, wpe, ln_w, ln_b, offs, out):
             bias.append(held.tile([P, 1], F32, name=f"bias{b}"))
             nc.sync.dma_start(position[b][:], wpe[rows, :])
             nc.sync.dma_start(table[b][:], wte[rows, :])
-            nc.gpsimd.dma_start(gain[b][:], ln_w[rows, :])
-            nc.gpsimd.dma_start(bias[b][:], ln_b[rows, :])
+            nc.scalar.dma_start(gain[b][:], ln_w[rows, :])
+            nc.scalar.dma_start(bias[b][:], ln_b[rows, :])
 
         averager = held.tile([P, P], F32, name="averager")
-        nc.vector.memset(averager[:], 1.0 / C)
+        nc.gpsimd.memset(averager[:], 1.0 / C)
+        averager_bf16 = held.tile([P, P], BF16, name="averager_bf16")
+        nc.gpsimd.memset(averager_bf16[:], 1.0 / C)
 
-        mean = psum.tile([P, N], F32, name="mean")
-        h = []
-        for b in range(BLOCKS):
-            h.append(held.tile([P, N], F32, name=f"h{b}"))
-            nc.vector.tensor_tensor(h[b][:], table[b][:].indirect(offsets[:]), position[b][:], ALU.add)
-            nc.tensor.matmul(mean[:], averager[:], h[b][:], start=(b == 0), stop=(b == BLOCKS - 1))
+        scratch = held.tile([P, 1], F32, name="scratch")
+        nc.gpsimd.memset(scratch[:], 1.0)
+        nc.scalar.activation(scratch[:], scratch[:], ACT.Abs_reciprocal_sqrt)
 
-        variance = psum.tile([P, N], F32, name="variance")
-        centred = []
+        h = [held.tile([P, BLOCKS, T], F32, name=f"h{p}") for p in range(PIECES)]
+        mean = [mean_banks.tile([P, T], F32, name=f"mean{p}") for p in range(PIECES)]
         for b in range(BLOCKS):
-            centred.append(held.tile([P, N], F32, name=f"centred{b}"))
-            squared = held.tile([P, N], F32, name=f"squared{b}")
-            nc.vector.tensor_tensor(centred[b][:], h[b][:], mean[:], ALU.subtract)
-            nc.scalar.activation(squared[:], centred[b][:], ACT.Square)
-            nc.tensor.matmul(variance[:], averager[:], squared[:], start=(b == 0), stop=(b == BLOCKS - 1))
+            for p in range(PIECES):
+                looked_up = table[b][:].indirect(offsets[:, p * (T // 16) : (p + 1) * (T // 16)])
+                nc.vector.tensor_tensor(h[p][:, b, :], looked_up, position[b][:, p * T : (p + 1) * T], ALU.add)
+                nc.tensor.matmul(mean[p][:], averager[:], h[p][:, b, :], start=(b == 0), stop=(b == BLOCKS - 1))
 
-        rstd = held.tile([P, N], F32, name="rstd")
-        nc.scalar.activation(rstd[:], variance[:], ACT.Abs_reciprocal_sqrt, bias=EPS)
-        for b in range(BLOCKS):
-            normed = held.tile([P, N], F32, name=f"normed{b}")
-            result = held.tile([P, N], F32, name=f"result{b}")
-            nc.vector.tensor_tensor(normed[:], centred[b][:], rstd[:], ALU.mult)
-            nc.scalar.activation(result[:], normed[:], ACT.Identity, bias=bias[b][:], scale=gain[b][:])
-            nc.sync.dma_start(out[b * P : (b + 1) * P, :], result[:])
+        out_blocks = out.rearrange("(b c) j -> c b j", b=BLOCKS)
+        for p in range(PIECES):
+            centred = work.tile([P, BLOCKS, T], F32)
+            nc.vector.tensor_tensor(
+                centred[:], h[p][:], mean[p][:].unsqueeze(1).to_broadcast([P, BLOCKS, T]), ALU.subtract
+            )
+            squared = work.tile([P, BLOCKS, T], BF16)
+            nc.scalar.activation(squared[:], centred[:], ACT.Square)
+            variance = variance_banks.tile([P, T], F32)
+            for b in range(BLOCKS):
+                nc.tensor.matmul(
+                    variance[:], averager_bf16[:], squared[:, b, :], start=(b == 0), stop=(b == BLOCKS - 1)
+                )
+            rstd = work.tile([P, T], F32)
+            nc.scalar.activation(rstd[:], variance[:], ACT.Abs_reciprocal_sqrt, bias=EPS)
+
+            normed = work.tile([P, BLOCKS, T], F32)
+            nc.vector.tensor_tensor(
+                normed[:], centred[:], rstd[:].unsqueeze(1).to_broadcast([P, BLOCKS, T]), ALU.mult
+            )
+            result = work.tile([P, BLOCKS, T], F32)
+            nc.scalar.activation(result[:, 0, :], normed[:, 0, :], ACT.Identity, bias=bias[0][:], scale=gain[0][:])
+            nc.vector.tensor_scalar(result[:, 1, :], normed[:, 1, :], gain[1][:], bias[1][:], ALU.mult, ALU.add)
+            nc.sync.dma_start(out_blocks[:, :, p * T : (p + 1) * T], result[:])

@@ -33,9 +33,11 @@ def tile_gptqbigcodemodel_kernel(tc, wte, wpe, ln_w, ln_b, offs, out):
             gain.append(held.tile([P, 1], F32, name=f"gain{b}"))
             bias.append(held.tile([P, 1], F32, name=f"bias{b}"))
             nc.sync.dma_start(position[b][:], wpe[rows, :])
-            nc.sync.dma_start(table[b][:], wte[rows, :])
             nc.scalar.dma_start(gain[b][:], ln_w[rows, :])
             nc.scalar.dma_start(bias[b][:], ln_b[rows, :])
+        nc.sync.dma_start(table[1][:, : S // 2], wte[P:, : S // 2])
+        nc.sync.dma_start(table[0][:], wte[:P, :])
+        nc.sync.dma_start(table[1][:, S // 2 :], wte[P:, S // 2 :])
 
         averager = held.tile([P, P], F32, name="averager")
         nc.gpsimd.memset(averager[:], 1.0 / C)
@@ -75,6 +77,8 @@ def tile_gptqbigcodemodel_kernel(tc, wte, wpe, ln_w, ln_b, offs, out):
                 normed[:], centred[:], rstd[:].unsqueeze(1).to_broadcast([P, BLOCKS, T]), ALU.mult
             )
             result = work.tile([P, BLOCKS, T], F32)
-            nc.scalar.activation(result[:, 0, :], normed[:, 0, :], ACT.Identity, bias=bias[0][:], scale=gain[0][:])
-            nc.vector.tensor_scalar(result[:, 1, :], normed[:, 1, :], gain[1][:], bias[1][:], ALU.mult, ALU.add)
+            for b in range(BLOCKS):
+                nc.scalar.activation(
+                    result[:, b, :], normed[:, b, :], ACT.Identity, bias=bias[b][:], scale=gain[b][:]
+                )
             nc.sync.dma_start(out_blocks[:, :, p * T : (p + 1) * T], result[:])

@@ -77,8 +77,6 @@ def tile_gptqbigcodemodel_kernel(tc, wte, wpe, ln_w, ln_b, offs, out):
                 normed[:], centred[:], rstd[:].unsqueeze(1).to_broadcast([P, BLOCKS, T]), ALU.mult
             )
             result = work.tile([P, BLOCKS, T], F32)
-            for b in range(BLOCKS):
-                nc.scalar.activation(
-                    result[:, b, :], normed[:, b, :], ACT.Identity, bias=bias[b][:], scale=gain[b][:]
-                )
+            nc.scalar.activation(result[:, 0, :], normed[:, 0, :], ACT.Identity, bias=bias[0][:], scale=gain[0][:])
+            nc.vector.tensor_scalar(result[:, 1, :], normed[:, 1, :], gain[1][:], bias[1][:], ALU.mult, ALU.add)
             nc.sync.dma_start(out_blocks[:, :, p * T : (p + 1) * T], result[:])

@@ -21,20 +21,19 @@ def tile_gptqbigcodemodel_kernel(tc, wte, wpe, ln_w, ln_b, offs, out):
         tc.tile_pool(name="held", bufs=1) as held,
         tc.tile_pool(name="work", bufs=PIECES) as work,
         tc.psum_pool(name="mean_banks", bufs=1) as mean_banks,
-        tc.psum_pool(name="variance_banks", bufs=PIECES) as variance_banks,
+        tc.psum_pool(name="variance_banks", bufs=PIECES - 1) as variance_banks,
+        tc.psum_pool(name="column_bank", bufs=1) as column_bank,
     ):
         offsets = held.tile([P, N // 16], U16, name="offsets")
         nc.sync.dma_start(offsets[:], offs)
-        position, table, gain, bias = [], [], [], []
+        position, table = [], []
         for b in range(BLOCKS):
-            rows = slice(b * P, (b + 1) * P)
             position.append(held.tile([P, N], F32, name=f"position{b}"))
             table.append(held.tile([P, S], F32, name=f"table{b}"))
-            gain.append(held.tile([P, 1], F32, name=f"gain{b}"))
-            bias.append(held.tile([P, 1], F32, name=f"bias{b}"))
-            nc.sync.dma_start(position[b][:], wpe[rows, :])
-            nc.scalar.dma_start(gain[b][:], ln_w[rows, :])
-            nc.scalar.dma_start(bias[b][:], ln_b[rows, :])
+            nc.sync.dma_start(position[b][:], wpe[b * P : (b + 1) * P, :])
+        gain_bias_rows = held.tile([1, 2 * C], F32, name="gain_bias_rows")
+        nc.scalar.dma_start(gain_bias_rows[:, :C], ln_w.rearrange("c x -> x c"))
+        nc.scalar.dma_start(gain_bias_rows[:, C:], ln_b.rearrange("c x -> x c"))
         nc.sync.dma_start(table[1][:, : S // 2], wte[P:, : S // 2])
         nc.sync.dma_start(table[0][:], wte[:P, :])
         nc.sync.dma_start(table[1][:, S // 2 :], wte[P:, S // 2 :])
@@ -43,6 +42,16 @@ def tile_gptqbigcodemodel_kernel(tc, wte, wpe, ln_w, ln_b, offs, out):
         nc.gpsimd.memset(averager[:], 1.0 / C)
         averager_bf16 = held.tile([P, P], BF16, name="averager_bf16")
         nc.gpsimd.memset(averager_bf16[:], 1.0 / C)
+
+        one = held.tile([1, 1], F32, name="one")
+        nc.gpsimd.memset(one[:], 1.0)
+        stood_up = column_bank.tile([P, 2 * BLOCKS], F32, name="stood_up")
+        for k in range(2 * BLOCKS):
+            nc.tensor.matmul(stood_up[:, k : k + 1], gain_bias_rows[:, k * P : (k + 1) * P], one[:], start=True, stop=True)
+        gain_bias = held.tile([P, 2 * BLOCKS], F32, name="gain_bias")
+        nc.vector.tensor_copy(gain_bias[:], stood_up[:])
+        gain = [gain_bias[:, b : b + 1] for b in range(BLOCKS)]
+        bias = [gain_bias[:, BLOCKS + b : BLOCKS + b + 1] for b in range(BLOCKS)]
 
         scratch = held.tile([P, 1], F32, name="scratch")
         nc.gpsimd.memset(scratch[:], 1.0)
@@ -77,6 +86,6 @@ def tile_gptqbigcodemodel_kernel(tc, wte, wpe, ln_w, ln_b, offs, out):
                 normed[:], centred[:], rstd[:].unsqueeze(1).to_broadcast([P, BLOCKS, T]), ALU.mult
             )
             result = work.tile([P, BLOCKS, T], F32)
-            nc.scalar.activation(result[:, 0, :], normed[:, 0, :], ACT.Identity, bias=bias[0][:], scale=gain[0][:])
-            nc.vector.tensor_scalar(result[:, 1, :], normed[:, 1, :], gain[1][:], bias[1][:], ALU.mult, ALU.add)
+            nc.scalar.activation(result[:, 0, :], normed[:, 0, :], ACT.Identity, bias=bias[0], scale=gain[0])
+            nc.vector.tensor_scalar(result[:, 1, :], normed[:, 1, :], gain[1], bias[1], ALU.mult, ALU.add)
             nc.sync.dma_start(out_blocks[:, :, p * T : (p + 1) * T], result[:])

@@ -21,7 +21,7 @@ def tile_gptqbigcodemodel_kernel(tc, wte, wpe, ln_w, ln_b, offs, out):
         tc.tile_pool(name="held", bufs=1) as held,
         tc.tile_pool(name="work", bufs=PIECES) as work,
         tc.psum_pool(name="mean_banks", bufs=1) as mean_banks,
-        tc.psum_pool(name="variance_banks", bufs=PIECES - 1) as variance_banks,
+        tc.psum_pool(name="short_banks", bufs=PIECES - 1) as short_banks,
         tc.psum_pool(name="column_bank", bufs=1) as column_bank,
     ):
         offsets = held.tile([P, N // 16], U16, name="offsets")
@@ -34,14 +34,17 @@ def tile_gptqbigcodemodel_kernel(tc, wte, wpe, ln_w, ln_b, offs, out):
         gain_bias_rows = held.tile([1, 2 * C], F32, name="gain_bias_rows")
         nc.scalar.dma_start(gain_bias_rows[:, :C], ln_w.rearrange("c x -> x c"))
         nc.scalar.dma_start(gain_bias_rows[:, C:], ln_b.rearrange("c x -> x c"))
-        nc.sync.dma_start(table[1][:, : S // 2], wte[P:, : S // 2])
-        nc.sync.dma_start(table[0][:], wte[:P, :])
-        nc.sync.dma_start(table[1][:, S // 2 :], wte[P:, S // 2 :])
+        for b in range(BLOCKS):
+            nc.sync.dma_start(table[b][:], wte[b * P : (b + 1) * P, :])
 
+        block_averager = held.tile([P, P], F32, name="block_averager")
+        nc.gpsimd.memset(block_averager[:], 1.0 / P)
         averager = held.tile([P, P], F32, name="averager")
         nc.gpsimd.memset(averager[:], 1.0 / C)
         averager_bf16 = held.tile([P, P], BF16, name="averager_bf16")
         nc.gpsimd.memset(averager_bf16[:], 1.0 / C)
+        minus_one_row = held.tile([P, P], BF16, name="minus_one_row")
+        nc.gpsimd.memset(minus_one_row[:], -1.0 / P)
 
         one = held.tile([1, 1], F32, name="one")
         nc.gpsimd.memset(one[:], 1.0)
@@ -57,33 +60,53 @@ def tile_gptqbigcodemodel_kernel(tc, wte, wpe, ln_w, ln_b, offs, out):
         nc.gpsimd.memset(scratch[:], 1.0)
         nc.scalar.activation(scratch[:], scratch[:], ACT.Abs_reciprocal_sqrt)
 
-        h = [held.tile([P, BLOCKS, T], F32, name=f"h{p}") for p in range(PIECES)]
+        def piece_of_list(p):
+            return offsets[:, p * (T // 16) : (p + 1) * (T // 16)]
+
+        d = [held.tile([P, BLOCKS, T], F32, name=f"d{p}") for p in range(PIECES)]
+        squared = [held.tile([P, BLOCKS, T], BF16, name=f"squared{p}") for p in range(PIECES)]
+        shifted_position = [held.tile([P, T], F32, name=f"shifted_position{p}") for p in range(PIECES)]
         mean = [mean_banks.tile([P, T], F32, name=f"mean{p}") for p in range(PIECES)]
-        for b in range(BLOCKS):
-            for p in range(PIECES):
-                looked_up = table[b][:].indirect(offsets[:, p * (T // 16) : (p + 1) * (T // 16)])
-                nc.vector.tensor_tensor(h[p][:, b, :], looked_up, position[b][:, p * T : (p + 1) * T], ALU.add)
-                nc.tensor.matmul(mean[p][:], averager[:], h[p][:, b, :], start=(b == 0), stop=(b == BLOCKS - 1))
+
+        for p in range(PIECES):
+            h_first = work.tile([P, T], F32)
+            nc.vector.tensor_tensor(
+                h_first[:], table[0][:].indirect(piece_of_list(p)), position[0][:, p * T : (p + 1) * T], ALU.add
+            )
+            shift = short_banks.tile([P, T], F32, tag="short")
+            nc.tensor.matmul(shift[:], block_averager[:], h_first[:], start=True, stop=True)
+            nc.vector.tensor_tensor(shifted_position[p][:], position[1][:, p * T : (p + 1) * T], shift[:], ALU.subtract)
+            nc.vector.tensor_tensor(d[p][:, 0, :], h_first[:], shift[:], ALU.subtract)
+            nc.tensor.matmul(mean[p][:], averager[:], d[p][:, 0, :], start=True, stop=False)
+            nc.scalar.activation(squared[p][:, 0, :], d[p][:, 0, :], ACT.Square)
+
+        for p in range(PIECES):
+            nc.vector.tensor_tensor(
+                d[p][:, 1, :], table[1][:].indirect(piece_of_list(p)), shifted_position[p][:], ALU.add
+            )
+            nc.tensor.matmul(mean[p][:], averager[:], d[p][:, 1, :], start=False, stop=True)
+            nc.scalar.activation(squared[p][:, 1, :], d[p][:, 1, :], ACT.Square)
+
+        rstd, centred = [], []
+        for p in range(PIECES):
+            mean_squared = work.tile([P, T], BF16)
+            nc.scalar.activation(mean_squared[:], mean[p][:], ACT.Square)
+            variance = short_banks.tile([P, T], F32, tag="short")
+            for b in range(BLOCKS):
+                nc.tensor.matmul(variance[:], averager_bf16[:], squared[p][:, b, :], start=(b == 0), stop=False)
+            nc.tensor.matmul(variance[:], minus_one_row[:], mean_squared[:], start=False, stop=True)
+            rstd.append(work.tile([P, T], F32, name="rstd"))
+            nc.scalar.activation(rstd[p][:], variance[:], ACT.Abs_reciprocal_sqrt, bias=EPS)
+            centred.append(work.tile([P, BLOCKS, T], F32, name="centred"))
+            nc.vector.tensor_tensor(
+                centred[p][:], d[p][:], mean[p][:].unsqueeze(1).to_broadcast([P, BLOCKS, T]), ALU.subtract
+            )
 
         out_blocks = out.rearrange("(b c) j -> c b j", b=BLOCKS)
         for p in range(PIECES):
-            centred = work.tile([P, BLOCKS, T], F32)
-            nc.vector.tensor_tensor(
-                centred[:], h[p][:], mean[p][:].unsqueeze(1).to_broadcast([P, BLOCKS, T]), ALU.subtract
-            )
-            squared = work.tile([P, BLOCKS, T], BF16)
-            nc.scalar.activation(squared[:], centred[:], ACT.Square)
-            variance = variance_banks.tile([P, T], F32)
-            for b in range(BLOCKS):
-                nc.tensor.matmul(
-                    variance[:], averager_bf16[:], squared[:, b, :], start=(b == 0), stop=(b == BLOCKS - 1)
-                )
-            rstd = work.tile([P, T], F32)
-            nc.scalar.activation(rstd[:], variance[:], ACT.Abs_reciprocal_sqrt, bias=EPS)
-
             normed = work.tile([P, BLOCKS, T], F32)
             nc.vector.tensor_tensor(
-                normed[:], centred[:], rstd[:].unsqueeze(1).to_broadcast([P, BLOCKS, T]), ALU.mult
+                normed[:], centred[p][:], rstd[p][:].unsqueeze(1).to_broadcast([P, BLOCKS, T]), ALU.mult
             )
             result = work.tile([P, BLOCKS, T], F32)
             nc.scalar.activation(result[:, 0, :], normed[:, 0, :], ACT.Identity, bias=bias[0], scale=gain[0])

@@ -7,6 +7,7 @@ ALU = mybir.AluOpType
 ACT = mybir.ActivationFunctionType
 
 P = 128
+LINE = 256
 C, S, N = 256, 4096, 512
 BLOCKS = C // P
 PIECES = 4
@@ -24,12 +25,12 @@ def tile_gptqbigcodemodel_kernel(tc, wte, wpe, ln_w, ln_b, offs, out):
         tc.psum_pool(name="short_banks", bufs=PIECES - 1) as short_banks,
         tc.psum_pool(name="column_bank", bufs=1) as column_bank,
     ):
-        offsets = held.tile([P, N // 16], U16, name="offsets")
+        offsets = held.tile([P, N // 16], U16, name="offsets", align_bytes=LINE)
         nc.sync.dma_start(offsets[:], offs)
         position, table = [], []
         for b in range(BLOCKS):
-            position.append(held.tile([P, N], F32, name=f"position{b}"))
-            table.append(held.tile([P, S], F32, name=f"table{b}"))
+            position.append(held.tile([P, N], F32, name=f"position{b}", align_bytes=LINE))
+            table.append(held.tile([P, S], F32, name=f"table{b}", align_bytes=LINE))
             nc.sync.dma_start(position[b][:], wpe[b * P : (b + 1) * P, :])
         gain_bias_rows = held.tile([1, 2 * C], F32, name="gain_bias_rows")
         nc.scalar.dma_start(gain_bias_rows[:, :C], ln_w.rearrange("c x -> x c"))
@@ -108,7 +109,7 @@ def tile_gptqbigcodemodel_kernel(tc, wte, wpe, ln_w, ln_b, offs, out):
             nc.vector.tensor_tensor(
                 normed[:], centred[p][:], rstd[p][:].unsqueeze(1).to_broadcast([P, BLOCKS, T]), ALU.mult
             )
-            result = work.tile([P, BLOCKS, T], F32)
+            result = work.tile([P, BLOCKS, T], F32, align_bytes=LINE)
             nc.scalar.activation(result[:, 0, :], normed[:, 0, :], ACT.Identity, bias=bias[0], scale=gain[0])
             nc.vector.tensor_scalar(result[:, 1, :], normed[:, 1, :], gain[1], bias[1], ALU.mult, ALU.add)
             nc.sync.dma_start(out_blocks[:, :, p * T : (p + 1) * T], result[:])

@@ -105,11 +105,21 @@ def tile_gptqbigcodemodel_kernel(tc, wte, wpe, ln_w, ln_b, offs, out):
 
         out_blocks = out.rearrange("(b c) j -> c b j", b=BLOCKS)
         for p in range(PIECES):
+            here = slice(p * T, (p + 1) * T)
             normed = work.tile([P, BLOCKS, T], F32)
-            nc.vector.tensor_tensor(
-                normed[:], centred[p][:], rstd[p][:].unsqueeze(1).to_broadcast([P, BLOCKS, T]), ALU.mult
-            )
             result = work.tile([P, BLOCKS, T], F32, align_bytes=LINE)
+            groups = [slice(0, BLOCKS)] if p < PIECES - 1 else [slice(b, b + 1) for b in range(BLOCKS)]
+            for g in groups:
+                nc.vector.tensor_tensor(
+                    normed[:, g, :],
+                    centred[p][:, g, :],
+                    rstd[p][:].unsqueeze(1).to_broadcast([P, g.stop - g.start, T]),
+                    ALU.mult,
+                )
             nc.scalar.activation(result[:, 0, :], normed[:, 0, :], ACT.Identity, bias=bias[0], scale=gain[0])
-            nc.vector.tensor_scalar(result[:, 1, :], normed[:, 1, :], gain[1], bias[1], ALU.mult, ALU.add)
-            nc.sync.dma_start(out_blocks[:, :, p * T : (p + 1) * T], result[:])
+            if p < PIECES - 1:
+                nc.scalar.activation(result[:, 1, :], normed[:, 1, :], ACT.Identity, bias=bias[1], scale=gain[1])
+            else:
+                nc.vector.tensor_scalar(result[:, 1, :], normed[:, 1, :], gain[1], bias[1], ALU.mult, ALU.add)
+            for g in groups:
+                nc.sync.dma_start(out_blocks[:, g, here], result[:, g, :])

@@ -108,18 +108,13 @@ def tile_gptqbigcodemodel_kernel(tc, wte, wpe, ln_w, ln_b, offs, out):
             here = slice(p * T, (p + 1) * T)
             normed = work.tile([P, BLOCKS, T], F32)
             result = work.tile([P, BLOCKS, T], F32, align_bytes=LINE)
-            groups = [slice(0, BLOCKS)] if p < PIECES - 1 else [slice(b, b + 1) for b in range(BLOCKS)]
-            for g in groups:
-                nc.vector.tensor_tensor(
-                    normed[:, g, :],
-                    centred[p][:, g, :],
-                    rstd[p][:].unsqueeze(1).to_broadcast([P, g.stop - g.start, T]),
-                    ALU.mult,
-                )
+            for b in range(BLOCKS):
+                nc.vector.tensor_tensor(normed[:, b, :], centred[p][:, b, :], rstd[p][:], ALU.mult)
             nc.scalar.activation(result[:, 0, :], normed[:, 0, :], ACT.Identity, bias=bias[0], scale=gain[0])
             if p < PIECES - 1:
                 nc.scalar.activation(result[:, 1, :], normed[:, 1, :], ACT.Identity, bias=bias[1], scale=gain[1])
             else:
                 nc.vector.tensor_scalar(result[:, 1, :], normed[:, 1, :], gain[1], bias[1], ALU.mult, ALU.add)
-            for g in groups:
-                nc.sync.dma_start(out_blocks[:, g, here], result[:, g, :])
+            stores = [slice(0, BLOCKS)] if p < PIECES - 1 else [slice(b, b + 1) for b in range(BLOCKS)]
+            for blocks in stores:
+                nc.sync.dma_start(out_blocks[:, blocks, here], result[:, blocks, :])

import concourse.mybir as mybir

F32 = mybir.dt.float32
BF16 = mybir.dt.bfloat16
U16 = mybir.dt.uint16
ALU = mybir.AluOpType
ACT = mybir.ActivationFunctionType

P = 128
LINE = 256
C, S, N = 256, 4096, 512
BLOCKS = C // P
PIECES = 4
T = N // PIECES
EPS = 1e-5
FLOPS = 8 * C * N


def tile_gptqbigcodemodel_kernel(tc, wte, wpe, ln_w, ln_b, offs, out):
    nc = tc.nc
    with (
        tc.tile_pool(name="held", bufs=1) as held,
        tc.tile_pool(name="work", bufs=PIECES) as work,
        tc.psum_pool(name="mean_banks", bufs=1) as mean_banks,
        tc.psum_pool(name="short_banks", bufs=PIECES - 1) as short_banks,
        tc.psum_pool(name="column_bank", bufs=1) as column_bank,
    ):
        offsets = held.tile([P, N // 16], U16, name="offsets", align_bytes=LINE)
        nc.sync.dma_start(offsets[:], offs)
        position, table = [], []
        for b in range(BLOCKS):
            position.append(held.tile([P, N], F32, name=f"position{b}", align_bytes=LINE))
            table.append(held.tile([P, S], F32, name=f"table{b}", align_bytes=LINE))
            nc.sync.dma_start(position[b][:], wpe[b * P : (b + 1) * P, :])
        gain_bias_rows = held.tile([1, 2 * C], F32, name="gain_bias_rows")
        nc.scalar.dma_start(gain_bias_rows[:, :C], ln_w.rearrange("c x -> x c"))
        nc.scalar.dma_start(gain_bias_rows[:, C:], ln_b.rearrange("c x -> x c"))
        for b in range(BLOCKS):
            nc.sync.dma_start(table[b][:], wte[b * P : (b + 1) * P, :])

        block_averager = held.tile([P, P], F32, name="block_averager")
        nc.gpsimd.memset(block_averager[:], 1.0 / P)
        averager = held.tile([P, P], F32, name="averager")
        nc.gpsimd.memset(averager[:], 1.0 / C)
        averager_bf16 = held.tile([P, P], BF16, name="averager_bf16")
        nc.gpsimd.memset(averager_bf16[:], 1.0 / C)
        minus_one_row = held.tile([P, P], BF16, name="minus_one_row")
        nc.gpsimd.memset(minus_one_row[:], -1.0 / P)

        one = held.tile([1, 1], F32, name="one")
        nc.gpsimd.memset(one[:], 1.0)
        stood_up = column_bank.tile([P, 2 * BLOCKS], F32, name="stood_up")
        for k in range(2 * BLOCKS):
            nc.tensor.matmul(stood_up[:, k : k + 1], gain_bias_rows[:, k * P : (k + 1) * P], one[:], start=True, stop=True)
        gain_bias = held.tile([P, 2 * BLOCKS], F32, name="gain_bias")
        nc.vector.tensor_copy(gain_bias[:], stood_up[:])
        gain = [gain_bias[:, b : b + 1] for b in range(BLOCKS)]
        bias = [gain_bias[:, BLOCKS + b : BLOCKS + b + 1] for b in range(BLOCKS)]

        scratch = held.tile([P, 1], F32, name="scratch")
        nc.gpsimd.memset(scratch[:], 1.0)
        nc.scalar.activation(scratch[:], scratch[:], ACT.Abs_reciprocal_sqrt)

        def piece_of_list(p):
            return offsets[:, p * (T // 16) : (p + 1) * (T // 16)]

        d = [held.tile([P, BLOCKS, T], F32, name=f"d{p}") for p in range(PIECES)]
        squared = [held.tile([P, BLOCKS, T], BF16, name=f"squared{p}") for p in range(PIECES)]
        shifted_position = [held.tile([P, T], F32, name=f"shifted_position{p}") for p in range(PIECES)]
        mean = [mean_banks.tile([P, T], F32, name=f"mean{p}") for p in range(PIECES)]

        for p in range(PIECES):
            h_first = work.tile([P, T], F32)
            nc.vector.tensor_tensor(
                h_first[:], table[0][:].indirect(piece_of_list(p)), position[0][:, p * T : (p + 1) * T], ALU.add
            )
            shift = short_banks.tile([P, T], F32, tag="short")
            nc.tensor.matmul(shift[:], block_averager[:], h_first[:], start=True, stop=True)
            nc.vector.tensor_tensor(shifted_position[p][:], position[1][:, p * T : (p + 1) * T], shift[:], ALU.subtract)
            nc.vector.tensor_tensor(d[p][:, 0, :], h_first[:], shift[:], ALU.subtract)
            nc.tensor.matmul(mean[p][:], averager[:], d[p][:, 0, :], start=True, stop=False)
            nc.scalar.activation(squared[p][:, 0, :], d[p][:, 0, :], ACT.Square)

        for p in range(PIECES):
            nc.vector.tensor_tensor(
                d[p][:, 1, :], table[1][:].indirect(piece_of_list(p)), shifted_position[p][:], ALU.add
            )
            nc.tensor.matmul(mean[p][:], averager[:], d[p][:, 1, :], start=False, stop=True)
            nc.scalar.activation(squared[p][:, 1, :], d[p][:, 1, :], ACT.Square)

        rstd, centred = [], []
        for p in range(PIECES):
            mean_squared = work.tile([P, T], BF16)
            nc.scalar.activation(mean_squared[:], mean[p][:], ACT.Square)
            variance = short_banks.tile([P, T], F32, tag="short")
            for b in range(BLOCKS):
                nc.tensor.matmul(variance[:], averager_bf16[:], squared[p][:, b, :], start=(b == 0), stop=False)
            nc.tensor.matmul(variance[:], minus_one_row[:], mean_squared[:], start=False, stop=True)
            rstd.append(work.tile([P, T], F32, name="rstd"))
            nc.scalar.activation(rstd[p][:], variance[:], ACT.Abs_reciprocal_sqrt, bias=EPS)
            centred.append(work.tile([P, BLOCKS, T], F32, name="centred"))
            nc.vector.tensor_tensor(
                centred[p][:], d[p][:], mean[p][:].unsqueeze(1).to_broadcast([P, BLOCKS, T]), ALU.subtract
            )

        out_blocks = out.rearrange("(b c) j -> c b j", b=BLOCKS)
        for p in range(PIECES):
            here = slice(p * T, (p + 1) * T)
            normed = work.tile([P, BLOCKS, T], F32)
            result = work.tile([P, BLOCKS, T], F32, align_bytes=LINE)
            for b in range(BLOCKS):
                nc.vector.tensor_tensor(normed[:, b, :], centred[p][:, b, :], rstd[p][:], ALU.mult)
            nc.scalar.activation(result[:, 0, :], normed[:, 0, :], ACT.Identity, bias=bias[0], scale=gain[0])
            if p < PIECES - 1:
                nc.scalar.activation(result[:, 1, :], normed[:, 1, :], ACT.Identity, bias=bias[1], scale=gain[1])
            else:
                nc.vector.tensor_scalar(result[:, 1, :], normed[:, 1, :], gain[1], bias[1], ALU.mult, ALU.add)
            stores = [slice(0, BLOCKS)] if p < PIECES - 1 else [slice(b, b + 1) for b in range(BLOCKS)]
            for blocks in stores:
                nc.sync.dma_start(out_blocks[:, blocks, here], result[:, blocks, :])
